import numpy as np
import ml_dtypes


def mxq(x, axis, fmt="e4m3"):
    dtype, down = {"e4m3": (ml_dtypes.float8_e4m3fn, 7), "e5m2": (ml_dtypes.float8_e5m2, 14)}[fmt]
    v = np.moveaxis(np.asarray(x, np.float32).astype(ml_dtypes.bfloat16).astype(np.float64), axis, -1)
    blocks = v.reshape(v.shape[:-1] + (-1, 32))
    amax = np.abs(blocks).max(-1, keepdims=True)
    byte = np.maximum(np.where(amax > 0, np.frexp(amax)[1] - 1 + 127, 0) - down, 1)
    scale = np.exp2(byte - 127.0)
    codes = (blocks / scale).astype(np.float32).astype(dtype).astype(np.float64)
    return np.moveaxis((codes * scale).reshape(v.shape), -1, axis)


WIDE = False


def mx_kscale(k):
    if not WIDE:
        return np.ones(k)
    levels = np.array([10, -10, 5, -5, 0])
    a = np.random.permutation(np.resize(levels, k // 512 * 4)).reshape(k // 512, 4)
    idx = np.arange(k)
    return np.exp2(a[idx // 512, idx % 128 // 32])


BF16 = ml_dtypes.bfloat16


def bf(x):
    return np.asarray(x, np.float32).astype(BF16)


def f64(x):
    return np.asarray(x).astype(np.float64)


B, S, E, H, F = 4, 1024, 512, 4, 4096
DH = E // H


def rms_norm(x):
    ms = np.mean(np.square(x), axis=2, keepdims=True)
    return x / np.sqrt(ms)


def setup_inputs():
    s = mx_kscale(E)
    c = 2.0 ** np.round(np.log2(np.sqrt(np.mean(np.square(s)))))
    r = (c / s)[:, None, None]
    row = 0.5 + 1.5 * np.random.random((B, S, 1))
    return {'x': bf(np.random.standard_normal((B, S, E)) * row * s[None, None, :]),
            'w_q': bf(np.random.standard_normal((E, H, DH)) * 1.5 / np.sqrt(E) * r),
            'w_k': bf(np.random.standard_normal((E, H, DH)) * 1.5 / np.sqrt(E) * r),
            'w_v': bf(np.random.standard_normal((E, H, DH)) / np.sqrt(E) * r)}


def reference(x, w_q, w_k, w_v):
    xq = mxq(rms_norm(f64(x)), 2, 'e4m3')
    q = (xq @ mxq(f64(w_q).reshape(E, H * DH), 0, 'e4m3')).reshape(B, S, H, DH)
    k = (xq @ mxq(f64(w_k).reshape(E, H * DH), 0, 'e4m3')).reshape(B, S, H, DH)
    v = (xq @ mxq(f64(w_v).reshape(E, H * DH), 0, 'e4m3')).reshape(B, S, H, DH)
    return q, k, v

@@ -1,0 +1,159 @@
+from contextlib import ExitStack
+
+import concourse.mybir as mybir
+from concourse.masks import make_identity
+
+BF16 = mybir.dt.bfloat16
+F32 = mybir.dt.float32
+U32 = mybir.dt.uint32
+U8 = mybir.dt.uint8
+FP8X4 = mybir.dt.float8_e4m3fn_x4
+ACT = mybir.ActivationFunctionType
+ALU = mybir.AluOpType
+
+P = 128
+PACK = 4
+FEATURES = P * PACK
+TOKENS = 4 * 1024
+TILES = TOKENS // P
+GROUP = 4
+GROUPS = TILES // GROUP
+COLUMNS = 4 * 128
+PROJECTIONS = 3
+
+FLOPS = 2 * TOKENS * FEATURES * COLUMNS * PROJECTIONS
+
+
+def tile_encoder_pa_t_kernel(tc, x, w_q, w_k, w_v, out_0, out_1, out_2):
+    nc = tc.nc
+    x_tiles = x.rearrange("b (q j) e -> (b q) j e", j=TILES)
+    out_tiles = [
+        out.rearrange("b (q j) h d -> (b q) j (h d)", j=TILES)
+        for out in (out_0, out_1, out_2)
+    ]
+
+    with ExitStack() as ctx:
+        keep = ctx.enter_context(tc.tile_pool(name="keep", bufs=1))
+        x_pool = ctx.enter_context(tc.tile_pool(name="x", bufs=GROUPS))
+        w_pool = ctx.enter_context(tc.tile_pool(name="w", bufs=PROJECTIONS))
+        stat_pool = ctx.enter_context(tc.tile_pool(name="stat", bufs=3))
+        square_pool = ctx.enter_context(tc.tile_pool(name="square", bufs=4))
+        xn_pool = ctx.enter_context(tc.tile_pool(name="xn", bufs=3))
+        mx_pool = ctx.enter_context(tc.tile_pool(name="mx", bufs=3))
+        result_pool = ctx.enter_context(tc.tile_pool(name="result", bufs=4))
+        turned_pool = ctx.enter_context(tc.psum_pool(name="turned", bufs=2))
+        product_pool = ctx.enter_context(tc.psum_pool(name="product", bufs=6))
+
+        x_groups = []
+        w_raws = []
+
+        def load_x(g):
+            x_group = x_pool.tile([P, GROUP, FEATURES], BF16)
+            nc.sync.dma_start(out=x_group[:], in_=x_tiles[:, g * GROUP : (g + 1) * GROUP, :])
+            x_groups.append(x_group)
+
+        load_x(0)
+        for w in (w_q, w_k, w_v):
+            w_raw = w_pool.tile([P, PACK, COLUMNS], BF16)
+            nc.sync.dma_start(out=w_raw[:], in_=w.rearrange("(t p) h d -> p t (h d)", p=P))
+            w_raws.append(w_raw)
+        for g in range(1, GROUPS):
+            load_x(g)
+
+        identity = keep.tile([P, P], BF16)
+        make_identity(nc, identity[:])
+
+        w_codes = keep.tile([P, PROJECTIONS, COLUMNS], U32, align_bytes=64)
+        w_scales = keep.tile([P, PROJECTIONS, COLUMNS], U8, align_bytes=64)
+        w_groupeds = []
+        for w_raw in w_raws:
+            w_grouped = w_pool.tile([P, COLUMNS, PACK], BF16, align_bytes=64)
+            nc.vector.tensor_copy(out=w_grouped[:], in_=w_raw[:].rearrange("p t n -> p n t"))
+            w_groupeds.append(w_grouped)
+        for i, w_grouped in enumerate(w_groupeds):
+            nc.vector.quantize_mx(
+                out=w_codes[:, i, :].bitcast(FP8X4),
+                scales=w_scales[:, i, :],
+                in_=w_grouped[:].rearrange("p n t -> p (n t)"),
+            )
+
+        def normalise(g):
+            x_group = x_groups[g]
+            sum_squares = stat_pool.tile([P, GROUP], F32)
+            for j in range(GROUP):
+                squares = square_pool.tile([P, FEATURES], BF16)
+                nc.scalar.activation(
+                    out=squares[:],
+                    in_=x_group[:, j, :],
+                    func=ACT.Square,
+                    accum_out=sum_squares[:, j : j + 1],
+                )
+            rms = stat_pool.tile([P, GROUP], F32)
+            nc.scalar.activation(out=rms[:], in_=sum_squares[:], func=ACT.Sqrt, scale=1.0 / FEATURES)
+            inverse_rms = stat_pool.tile([P, GROUP], F32)
+            nc.vector.reciprocal(out=inverse_rms[:], in_=rms[:])
+            xn = xn_pool.tile([P, GROUP, FEATURES], BF16)
+            for j in range(GROUP):
+                nc.gpsimd.tensor_scalar(
+                    out=xn[:, j, :],
+                    in0=x_group[:, j, :],
+                    scalar1=inverse_rms[:, j : j + 1],
+                    scalar2=0.0,
+                    op0=ALU.mult,
+                    op1=ALU.add,
+                )
+            return xn
+
+        def turn_and_quantise(xn):
+            grouped = mx_pool.tile([P, GROUP, P, PACK], BF16, align_bytes=64)
+            for half in range(GROUP // 2):
+                turned = turned_pool.tile([P, 2, PACK, P], BF16)
+                for j in range(2):
+                    for t in range(PACK):
+                        nc.tensor.transpose(
+                            turned[:, j, t, :],
+                            xn[:, 2 * half + j, t * P : (t + 1) * P],
+                            identity[:],
+                        )
+                nc.vector.tensor_copy(
+                    out=grouped[:, 2 * half : 2 * half + 2, :, :],
+                    in_=turned[:].rearrange("p j t r -> p j r t"),
+                )
+            codes = mx_pool.tile([P, GROUP * P], U32, align_bytes=64)
+            scales = mx_pool.tile([P, GROUP * P], U8, align_bytes=64)
+            nc.vector.quantize_mx(
+                out=codes[:].bitcast(FP8X4),
+                scales=scales[:],
+                in_=grouped[:].rearrange("p j r t -> p (j r t)"),
+            )
+            return codes, scales
+
+        def project(g, codes, scales):
+            for i in range(PROJECTIONS):
+                result = result_pool.tile([P, GROUP, COLUMNS], F32, tag="result%d" % i)
+                for j in range(GROUP):
+                    tokens = slice(j * P, (j + 1) * P)
+                    product = product_pool.tile([P, COLUMNS], F32)
+                    nc.tensor.matmul_mx(
+                        out=product[:],
+                        lhsT=codes[:, tokens].bitcast(FP8X4),
+                        lhsT_scale=scales[:, tokens],
+                        rhs=w_codes[:, i, :].bitcast(FP8X4),
+                        rhs_scale=w_scales[:, i, :],
+                        start=True,
+                        stop=True,
+                    )
+                    nc.any.tensor_copy(out=result[:, j, :], in_=product[:])
+                nc.sync.dma_start(
+                    out=out_tiles[i][:, g * GROUP : (g + 1) * GROUP, :], in_=result[:]
+                )
+
+        xns = [normalise(0), normalise(1)]
+        quantised = [turn_and_quantise(xns[0])]
+        for g in range(GROUPS):
+            if g + 2 < GROUPS:
+                xns.append(normalise(g + 2))
+            if g + 1 < GROUPS:
+                quantised.append(turn_and_quantise(xns[g + 1]))
+            codes, scales = quantised[g]
+            project(g, codes, scales)

@@ -9,13 +9,14 @@ U32 = mybir.dt.uint32
 U8 = mybir.dt.uint8
 FP8X4 = mybir.dt.float8_e4m3fn_x4
 ACT = mybir.ActivationFunctionType
-ALU = mybir.AluOpType
 
 P = 128
 PACK = 4
 FEATURES = P * PACK
+HALVES = 2
 TOKENS = 4 * 1024
 TILES = TOKENS // P
+PAIR = 2
 GROUP = 4
 GROUPS = TILES // GROUP
 COLUMNS = 4 * 128
@@ -36,13 +37,18 @@ def tile_encoder_pa_t_kernel(tc, x, w_q, w_k, w_v, out_0, out_1, out_2):
         keep = ctx.enter_context(tc.tile_pool(name="keep", bufs=1))
         x_pool = ctx.enter_context(tc.tile_pool(name="x", bufs=GROUPS))
         w_pool = ctx.enter_context(tc.tile_pool(name="w", bufs=PROJECTIONS))
-        stat_pool = ctx.enter_context(tc.tile_pool(name="stat", bufs=3))
+        stat_pool = ctx.enter_context(tc.tile_pool(name="stat", bufs=6))
         square_pool = ctx.enter_context(tc.tile_pool(name="square", bufs=4))
-        xn_pool = ctx.enter_context(tc.tile_pool(name="xn", bufs=3))
-        mx_pool = ctx.enter_context(tc.tile_pool(name="mx", bufs=3))
+        xn_pool = ctx.enter_context(tc.tile_pool(name="xn", bufs=6))
+        mx_pool = ctx.enter_context(tc.tile_pool(name="mx", bufs=6))
         result_pool = ctx.enter_context(tc.tile_pool(name="result", bufs=4))
         turned_pool = ctx.enter_context(tc.psum_pool(name="turned", bufs=2))
         product_pool = ctx.enter_context(tc.psum_pool(name="product", bufs=6))
+
+        one = keep.tile([P, 1], F32)
+        nc.vector.memset(one[:], 1.0)
+        root_of_one = keep.tile([P, 1], F32)
+        nc.scalar.activation(out=root_of_one[:], in_=one[:], func=ACT.Sqrt)
 
         x_groups = []
         w_raws = []
@@ -55,72 +61,68 @@ def tile_encoder_pa_t_kernel(tc, x, w_q, w_k, w_v, out_0, out_1, out_2):
         load_x(0)
         for w in (w_q, w_k, w_v):
             w_raw = w_pool.tile([P, PACK, COLUMNS], BF16)
-            nc.sync.dma_start(out=w_raw[:], in_=w.rearrange("(t p) h d -> p t (h d)", p=P))
+            nc.sync.dma_start(
+                out=w_raw[:].rearrange("p (u e) n -> p u (e n)", u=HALVES),
+                in_=w.rearrange("(u p e) h d -> p u (e h d)", u=HALVES, p=P),
+            )
             w_raws.append(w_raw)
         for g in range(1, GROUPS):
             load_x(g)
 
-        identity = keep.tile([P, P], BF16)
+        identity = keep.tile([P, P], F32)
         make_identity(nc, identity[:])
 
-        w_codes = keep.tile([P, PROJECTIONS, COLUMNS], U32, align_bytes=64)
-        w_scales = keep.tile([P, PROJECTIONS, COLUMNS], U8, align_bytes=64)
-        w_groupeds = []
-        for w_raw in w_raws:
+        w_codes = []
+        w_scales = []
+
+        def prepare_weight(i):
             w_grouped = w_pool.tile([P, COLUMNS, PACK], BF16, align_bytes=64)
-            nc.vector.tensor_copy(out=w_grouped[:], in_=w_raw[:].rearrange("p t n -> p n t"))
-            w_groupeds.append(w_grouped)
-        for i, w_grouped in enumerate(w_groupeds):
+            nc.vector.tensor_copy(out=w_grouped[:], in_=w_raws[i][:].rearrange("p t n -> p n t"))
+            codes = w_pool.tile([P, COLUMNS], U32, align_bytes=64, name="w_codes")
+            scales = w_pool.tile([P, COLUMNS], U8, align_bytes=64, name="w_scales")
             nc.vector.quantize_mx(
-                out=w_codes[:, i, :].bitcast(FP8X4),
-                scales=w_scales[:, i, :],
+                out=codes[:].bitcast(FP8X4),
+                scales=scales[:],
                 in_=w_grouped[:].rearrange("p n t -> p (n t)"),
             )
+            w_codes.append(codes)
+            w_scales.append(scales)
 
-        def normalise(g):
-            x_group = x_groups[g]
-            sum_squares = stat_pool.tile([P, GROUP], F32)
-            for j in range(GROUP):
+        def normalise(pair):
+            x_group = x_groups[pair * PAIR // GROUP]
+            first = pair * PAIR % GROUP
+            sum_squares = stat_pool.tile([P, PAIR], F32)
+            for j in range(PAIR):
                 squares = square_pool.tile([P, FEATURES], BF16)
                 nc.scalar.activation(
                     out=squares[:],
-                    in_=x_group[:, j, :],
+                    in_=x_group[:, first + j, :],
                     func=ACT.Square,
                     accum_out=sum_squares[:, j : j + 1],
                 )
-            rms = stat_pool.tile([P, GROUP], F32)
+            rms = stat_pool.tile([P, PAIR], F32)
             nc.scalar.activation(out=rms[:], in_=sum_squares[:], func=ACT.Sqrt, scale=1.0 / FEATURES)
-            inverse_rms = stat_pool.tile([P, GROUP], F32)
+            inverse_rms = stat_pool.tile([P, PAIR], F32)
             nc.vector.reciprocal(out=inverse_rms[:], in_=rms[:])
-            xn = xn_pool.tile([P, GROUP, FEATURES], BF16)
-            for j in range(GROUP):
-                nc.gpsimd.tensor_scalar(
-                    out=xn[:, j, :],
-                    in0=x_group[:, j, :],
-                    scalar1=inverse_rms[:, j : j + 1],
-                    scalar2=0.0,
-                    op0=ALU.mult,
-                    op1=ALU.add,
+            xn = xn_pool.tile([P, PAIR, FEATURES], BF16)
+            for j in range(PAIR):
+                nc.vector.tensor_scalar_mul(
+                    out=xn[:, j, :], in0=x_group[:, first + j, :], scalar1=inverse_rms[:, j : j + 1]
                 )
             return xn
 
         def turn_and_quantise(xn):
-            grouped = mx_pool.tile([P, GROUP, P, PACK], BF16, align_bytes=64)
-            for half in range(GROUP // 2):
-                turned = turned_pool.tile([P, 2, PACK, P], BF16)
-                for j in range(2):
-                    for t in range(PACK):
-                        nc.tensor.transpose(
-                            turned[:, j, t, :],
-                            xn[:, 2 * half + j, t * P : (t + 1) * P],
-                            identity[:],
-                        )
-                nc.vector.tensor_copy(
-                    out=grouped[:, 2 * half : 2 * half + 2, :, :],
-                    in_=turned[:].rearrange("p j t r -> p j r t"),
-                )
-            codes = mx_pool.tile([P, GROUP * P], U32, align_bytes=64)
-            scales = mx_pool.tile([P, GROUP * P], U8, align_bytes=64)
+            turned = turned_pool.tile([P, PAIR, HALVES, P], F32)
+            for j in range(PAIR):
+                words = xn[:, j, :].bitcast(F32)
+                for u in range(HALVES):
+                    nc.tensor.transpose(turned[:, j, u, :], words[:, u * P : (u + 1) * P], identity[:])
+            grouped = mx_pool.tile([P, PAIR, P, PACK], BF16, align_bytes=64)
+            nc.vector.tensor_copy(
+                out=grouped[:].bitcast(F32), in_=turned[:].rearrange("p j u r -> p j r u")
+            )
+            codes = mx_pool.tile([P, PAIR * P], U32, align_bytes=64)
+            scales = mx_pool.tile([P, PAIR * P], U8, align_bytes=64)
             nc.vector.quantize_mx(
                 out=codes[:].bitcast(FP8X4),
                 scales=scales[:],
@@ -128,32 +130,42 @@ def tile_encoder_pa_t_kernel(tc, x, w_q, w_k, w_v, out_0, out_1, out_2):
             )
             return codes, scales
 
-        def project(g, codes, scales):
-            for i in range(PROJECTIONS):
-                result = result_pool.tile([P, GROUP, COLUMNS], F32, tag="result%d" % i)
-                for j in range(GROUP):
-                    tokens = slice(j * P, (j + 1) * P)
-                    product = product_pool.tile([P, COLUMNS], F32)
-                    nc.tensor.matmul_mx(
-                        out=product[:],
-                        lhsT=codes[:, tokens].bitcast(FP8X4),
-                        lhsT_scale=scales[:, tokens],
-                        rhs=w_codes[:, i, :].bitcast(FP8X4),
-                        rhs_scale=w_scales[:, i, :],
-                        start=True,
-                        stop=True,
-                    )
-                    nc.any.tensor_copy(out=result[:, j, :], in_=product[:])
-                nc.sync.dma_start(
-                    out=out_tiles[i][:, g * GROUP : (g + 1) * GROUP, :], in_=result[:]
+        def project(g, i):
+            result = result_pool.tile([P, GROUP, COLUMNS], F32, tag="result%d" % i)
+            for j in range(GROUP):
+                codes, scales = quantised[(g * GROUP + j) // PAIR]
+                tokens = slice(j % PAIR * P, (j % PAIR + 1) * P)
+                product = product_pool.tile([P, COLUMNS], F32)
+                nc.tensor.matmul_mx(
+                    out=product[:],
+                    lhsT=codes[:, tokens].bitcast(FP8X4),
+                    lhsT_scale=scales[:, tokens],
+                    rhs=w_codes[i][:].bitcast(FP8X4),
+                    rhs_scale=w_scales[i][:],
+                    start=True,
+                    stop=True,
                 )
+                if j % 2 == 0:
+                    nc.scalar.copy(out=result[:, j, :], in_=product[:])
+                else:
+                    nc.vector.tensor_copy(out=result[:, j, :], in_=product[:])
+            nc.sync.dma_start(out=out_tiles[i][:, g * GROUP : (g + 1) * GROUP, :], in_=result[:])
 
-        xns = [normalise(0), normalise(1)]
-        quantised = [turn_and_quantise(xns[0])]
+        pairs_in_group = GROUP // PAIR
+        xns = []
+        quantised = []
+        for pair in range(pairs_in_group):
+            xns.append(normalise(pair))
+            quantised.append(turn_and_quantise(xns[pair]))
+        for pair in range(pairs_in_group, 2 * pairs_in_group):
+            xns.append(normalise(pair))
         for g in range(GROUPS):
+            for i in range(PROJECTIONS):
+                if g == 0:
+                    prepare_weight(i)
+                project(g, i)
+                if i < pairs_in_group and g + 1 < GROUPS:
+                    quantised.append(turn_and_quantise(xns[(g + 1) * pairs_in_group + i]))
             if g + 2 < GROUPS:
-                xns.append(normalise(g + 2))
-            if g + 1 < GROUPS:
-                quantised.append(turn_and_quantise(xns[g + 1]))
-            codes, scales = quantised[g]
-            project(g, codes, scales)
+                for pair in range((g + 2) * pairs_in_group, (g + 3) * pairs_in_group):
+                    xns.append(normalise(pair))

@@ -77,7 +77,11 @@ def tile_encoder_pa_t_kernel(tc, x, w_q, w_k, w_v, out_0, out_1, out_2):
 
         def prepare_weight(i):
             w_grouped = w_pool.tile([P, COLUMNS, PACK], BF16, align_bytes=64)
-            nc.vector.tensor_copy(out=w_grouped[:], in_=w_raws[i][:].rearrange("p t n -> p n t"))
+            by_column = w_raws[i][:].rearrange("p t n -> p n t")
+            if i < PROJECTIONS - 1:
+                nc.vector.tensor_copy(out=w_grouped[:], in_=by_column)
+            else:
+                nc.scalar.copy(out=w_grouped[:], in_=by_column)
             codes = w_pool.tile([P, COLUMNS], U32, align_bytes=64, name="w_codes")
             scales = w_pool.tile([P, COLUMNS], U8, align_bytes=64, name="w_scales")
             nc.vector.quantize_mx(
@@ -152,20 +156,13 @@ def tile_encoder_pa_t_kernel(tc, x, w_q, w_k, w_v, out_0, out_1, out_2):
             nc.sync.dma_start(out=out_tiles[i][:, g * GROUP : (g + 1) * GROUP, :], in_=result[:])
 
         pairs_in_group = GROUP // PAIR
-        xns = []
         quantised = []
         for pair in range(pairs_in_group):
-            xns.append(normalise(pair))
-            quantised.append(turn_and_quantise(xns[pair]))
-        for pair in range(pairs_in_group, 2 * pairs_in_group):
-            xns.append(normalise(pair))
+            quantised.append(turn_and_quantise(normalise(pair)))
         for g in range(GROUPS):
             for i in range(PROJECTIONS):
                 if g == 0:
                     prepare_weight(i)
                 project(g, i)
                 if i < pairs_in_group and g + 1 < GROUPS:
-                    quantised.append(turn_and_quantise(xns[(g + 1) * pairs_in_group + i]))
-            if g + 2 < GROUPS:
-                for pair in range((g + 2) * pairs_in_group, (g + 3) * pairs_in_group):
-                    xns.append(normalise(pair))
+                    quantised.append(turn_and_quantise(normalise((g + 1) * pairs_in_group + i)))

@@ -9,6 +9,7 @@ U32 = mybir.dt.uint32
 U8 = mybir.dt.uint8
 FP8X4 = mybir.dt.float8_e4m3fn_x4
 ACT = mybir.ActivationFunctionType
+ALU = mybir.AluOpType
 
 P = 128
 PACK = 4
@@ -77,11 +78,7 @@ def tile_encoder_pa_t_kernel(tc, x, w_q, w_k, w_v, out_0, out_1, out_2):
 
         def prepare_weight(i):
             w_grouped = w_pool.tile([P, COLUMNS, PACK], BF16, align_bytes=64)
-            by_column = w_raws[i][:].rearrange("p t n -> p n t")
-            if i < PROJECTIONS - 1:
-                nc.vector.tensor_copy(out=w_grouped[:], in_=by_column)
-            else:
-                nc.scalar.copy(out=w_grouped[:], in_=by_column)
+            nc.vector.tensor_copy(out=w_grouped[:], in_=w_raws[i][:].rearrange("p t n -> p n t"))
             codes = w_pool.tile([P, COLUMNS], U32, align_bytes=64, name="w_codes")
             scales = w_pool.tile([P, COLUMNS], U8, align_bytes=64, name="w_scales")
             nc.vector.quantize_mx(
@@ -110,8 +107,13 @@ def tile_encoder_pa_t_kernel(tc, x, w_q, w_k, w_v, out_0, out_1, out_2):
             nc.vector.reciprocal(out=inverse_rms[:], in_=rms[:])
             xn = xn_pool.tile([P, PAIR, FEATURES], BF16)
             for j in range(PAIR):
-                nc.vector.tensor_scalar_mul(
-                    out=xn[:, j, :], in0=x_group[:, first + j, :], scalar1=inverse_rms[:, j : j + 1]
+                nc.gpsimd.tensor_scalar(
+                    out=xn[:, j, :],
+                    in0=x_group[:, first + j, :],
+                    scalar1=inverse_rms[:, j : j + 1],
+                    scalar2=0.0,
+                    op0=ALU.mult,
+                    op1=ALU.add,
                 )
             return xn
 
@@ -156,13 +158,20 @@ def tile_encoder_pa_t_kernel(tc, x, w_q, w_k, w_v, out_0, out_1, out_2):
             nc.sync.dma_start(out=out_tiles[i][:, g * GROUP : (g + 1) * GROUP, :], in_=result[:])
 
         pairs_in_group = GROUP // PAIR
+        xns = []
         quantised = []
         for pair in range(pairs_in_group):
-            quantised.append(turn_and_quantise(normalise(pair)))
+            xns.append(normalise(pair))
+            quantised.append(turn_and_quantise(xns[pair]))
+        for pair in range(pairs_in_group, 2 * pairs_in_group):
+            xns.append(normalise(pair))
         for g in range(GROUPS):
             for i in range(PROJECTIONS):
                 if g == 0:
                     prepare_weight(i)
                 project(g, i)
                 if i < pairs_in_group and g + 1 < GROUPS:
-                    quantised.append(turn_and_quantise(normalise((g + 1) * pairs_in_group + i)))
+                    quantised.append(turn_and_quantise(xns[(g + 1) * pairs_in_group + i]))
+            if g + 2 < GROUPS:
+                for pair in range((g + 2) * pairs_in_group, (g + 3) * pairs_in_group):
+                    xns.append(normalise(pair))

from contextlib import ExitStack

import concourse.mybir as mybir
from concourse.masks import make_identity

BF16 = mybir.dt.bfloat16
F32 = mybir.dt.float32
U32 = mybir.dt.uint32
U8 = mybir.dt.uint8
FP8X4 = mybir.dt.float8_e4m3fn_x4
ACT = mybir.ActivationFunctionType
ALU = mybir.AluOpType

P = 128
PACK = 4
FEATURES = P * PACK
HALVES = 2
TOKENS = 4 * 1024
TILES = TOKENS // P
PAIR = 2
GROUP = 4
GROUPS = TILES // GROUP
COLUMNS = 4 * 128
PROJECTIONS = 3

FLOPS = 2 * TOKENS * FEATURES * COLUMNS * PROJECTIONS


def tile_encoder_pa_t_kernel(tc, x, w_q, w_k, w_v, out_0, out_1, out_2):
    nc = tc.nc
    x_tiles = x.rearrange("b (q j) e -> (b q) j e", j=TILES)
    out_tiles = [
        out.rearrange("b (q j) h d -> (b q) j (h d)", j=TILES)
        for out in (out_0, out_1, out_2)
    ]

    with ExitStack() as ctx:
        keep = ctx.enter_context(tc.tile_pool(name="keep", bufs=1))
        x_pool = ctx.enter_context(tc.tile_pool(name="x", bufs=GROUPS))
        w_pool = ctx.enter_context(tc.tile_pool(name="w", bufs=PROJECTIONS))
        stat_pool = ctx.enter_context(tc.tile_pool(name="stat", bufs=6))
        square_pool = ctx.enter_context(tc.tile_pool(name="square", bufs=4))
        xn_pool = ctx.enter_context(tc.tile_pool(name="xn", bufs=6))
        mx_pool = ctx.enter_context(tc.tile_pool(name="mx", bufs=6))
        result_pool = ctx.enter_context(tc.tile_pool(name="result", bufs=4))
        turned_pool = ctx.enter_context(tc.psum_pool(name="turned", bufs=2))
        product_pool = ctx.enter_context(tc.psum_pool(name="product", bufs=6))

        one = keep.tile([P, 1], F32)
        nc.vector.memset(one[:], 1.0)
        root_of_one = keep.tile([P, 1], F32)
        nc.scalar.activation(out=root_of_one[:], in_=one[:], func=ACT.Sqrt)

        x_groups = []
        w_raws = []

        def load_x(g):
            x_group = x_pool.tile([P, GROUP, FEATURES], BF16)
            nc.sync.dma_start(out=x_group[:], in_=x_tiles[:, g * GROUP : (g + 1) * GROUP, :])
            x_groups.append(x_group)

        load_x(0)
        for w in (w_q, w_k, w_v):
            w_raw = w_pool.tile([P, PACK, COLUMNS], BF16)
            nc.sync.dma_start(
                out=w_raw[:].rearrange("p (u e) n -> p u (e n)", u=HALVES),
                in_=w.rearrange("(u p e) h d -> p u (e h d)", u=HALVES, p=P),
            )
            w_raws.append(w_raw)
        for g in range(1, GROUPS):
            load_x(g)

        identity = keep.tile([P, P], F32)
        make_identity(nc, identity[:])

        w_codes = []
        w_scales = []

        def prepare_weight(i):
            w_grouped = w_pool.tile([P, COLUMNS, PACK], BF16, align_bytes=64)
            nc.vector.tensor_copy(out=w_grouped[:], in_=w_raws[i][:].rearrange("p t n -> p n t"))
            codes = w_pool.tile([P, COLUMNS], U32, align_bytes=64, name="w_codes")
            scales = w_pool.tile([P, COLUMNS], U8, align_bytes=64, name="w_scales")
            nc.vector.quantize_mx(
                out=codes[:].bitcast(FP8X4),
                scales=scales[:],
                in_=w_grouped[:].rearrange("p n t -> p (n t)"),
            )
            w_codes.append(codes)
            w_scales.append(scales)

        def normalise(pair):
            x_group = x_groups[pair * PAIR // GROUP]
            first = pair * PAIR % GROUP
            sum_squares = stat_pool.tile([P, PAIR], F32)
            for j in range(PAIR):
                squares = square_pool.tile([P, FEATURES], BF16)
                nc.scalar.activation(
                    out=squares[:],
                    in_=x_group[:, first + j, :],
                    func=ACT.Square,
                    accum_out=sum_squares[:, j : j + 1],
                )
            rms = stat_pool.tile([P, PAIR], F32)
            nc.scalar.activation(out=rms[:], in_=sum_squares[:], func=ACT.Sqrt, scale=1.0 / FEATURES)
            inverse_rms = stat_pool.tile([P, PAIR], F32)
            nc.vector.reciprocal(out=inverse_rms[:], in_=rms[:])
            xn = xn_pool.tile([P, PAIR, FEATURES], BF16)
            for j in range(PAIR):
                nc.gpsimd.tensor_scalar(
                    out=xn[:, j, :],
                    in0=x_group[:, first + j, :],
                    scalar1=inverse_rms[:, j : j + 1],
                    scalar2=0.0,
                    op0=ALU.mult,
                    op1=ALU.add,
                )
            return xn

        def turn_and_quantise(xn):
            turned = turned_pool.tile([P, PAIR, HALVES, P], F32)
            for j in range(PAIR):
                words = xn[:, j, :].bitcast(F32)
                for u in range(HALVES):
                    nc.tensor.transpose(turned[:, j, u, :], words[:, u * P : (u + 1) * P], identity[:])
            grouped = mx_pool.tile([P, PAIR, P, PACK], BF16, align_bytes=64)
            nc.vector.tensor_copy(
                out=grouped[:].bitcast(F32), in_=turned[:].rearrange("p j u r -> p j r u")
            )
            codes = mx_pool.tile([P, PAIR * P], U32, align_bytes=64)
            scales = mx_pool.tile([P, PAIR * P], U8, align_bytes=64)
            nc.vector.quantize_mx(
                out=codes[:].bitcast(FP8X4),
                scales=scales[:],
                in_=grouped[:].rearrange("p j r t -> p (j r t)"),
            )
            return codes, scales

        def project(g, i):
            result = result_pool.tile([P, GROUP, COLUMNS], F32, tag="result%d" % i)
            for j in range(GROUP):
                codes, scales = quantised[(g * GROUP + j) // PAIR]
                tokens = slice(j % PAIR * P, (j % PAIR + 1) * P)
                product = product_pool.tile([P, COLUMNS], F32)
                nc.tensor.matmul_mx(
                    out=product[:],
                    lhsT=codes[:, tokens].bitcast(FP8X4),
                    lhsT_scale=scales[:, tokens],
                    rhs=w_codes[i][:].bitcast(FP8X4),
                    rhs_scale=w_scales[i][:],
                    start=True,
                    stop=True,
                )
                if j % 2 == 0:
                    nc.scalar.copy(out=result[:, j, :], in_=product[:])
                else:
                    nc.vector.tensor_copy(out=result[:, j, :], in_=product[:])
            nc.sync.dma_start(out=out_tiles[i][:, g * GROUP : (g + 1) * GROUP, :], in_=result[:])

        pairs_in_group = GROUP // PAIR
        xns = []
        quantised = []
        for pair in range(pairs_in_group):
            xns.append(normalise(pair))
            quantised.append(turn_and_quantise(xns[pair]))
        for pair in range(pairs_in_group, 2 * pairs_in_group):
            xns.append(normalise(pair))
        for g in range(GROUPS):
            for i in range(PROJECTIONS):
                if g == 0:
                    prepare_weight(i)
                project(g, i)
                if i < pairs_in_group and g + 1 < GROUPS:
                    quantised.append(turn_and_quantise(xns[(g + 1) * pairs_in_group + i]))
            if g + 2 < GROUPS:
                for pair in range((g + 2) * pairs_in_group, (g + 3) * pairs_in_group):
                    xns.append(normalise(pair))
